import numpy as np
import ml_dtypes


def mxq(x, axis, fmt="e4m3"):
    dtype, down = {"e4m3": (ml_dtypes.float8_e4m3fn, 7), "e5m2": (ml_dtypes.float8_e5m2, 14)}[fmt]
    v = np.moveaxis(np.asarray(x, np.float32).astype(ml_dtypes.bfloat16).astype(np.float64), axis, -1)
    blocks = v.reshape(v.shape[:-1] + (-1, 32))
    amax = np.abs(blocks).max(-1, keepdims=True)
    byte = np.maximum(np.where(amax > 0, np.frexp(amax)[1] - 1 + 127, 0) - down, 1)
    scale = np.exp2(byte - 127.0)
    codes = (blocks / scale).astype(np.float32).astype(dtype).astype(np.float64)
    return np.moveaxis((codes * scale).reshape(v.shape), -1, axis)


WIDE = False


def mx_kscale(k):
    if not WIDE:
        return np.ones(k)
    levels = np.array([10, -10, 5, -5, 0])
    if k % 512:
        return np.exp2(np.random.permutation(np.resize(levels, k // 32))).repeat(32)
    a = np.empty((k // 512, 16))
    for p in range(k // 512):
        a[p, :8] = np.random.permutation(np.resize(levels, 8))
        for g in range(8):
            far = levels[np.abs(levels - a[p, g]) >= 10]
            a[p, g + 8] = far[np.random.randint(len(far))]
    return np.exp2(a.ravel()).repeat(32)


BF16 = ml_dtypes.bfloat16


def bf(x):
    return np.asarray(x, np.float32).astype(BF16)


def f64(x):
    return np.asarray(x).astype(np.float64)


B_, S, D_IN, D_OUT, N, RANK, ALPHA = 1, 128, 512, 1024, 32, 16, 32
NR = N * RANK
SCALE = ALPHA / RANK


def setup_inputs():
    s, t = mx_kscale(D_IN), mx_kscale(NR)
    tn = t.reshape(N, RANK)
    return {"x": bf(np.random.standard_normal((B_, S, D_IN)) * s),
            "lora_A": bf(np.random.standard_normal((N, RANK, D_IN)) / np.sqrt(D_IN) / s * tn[:, :, None]),
            "lora_B": bf(np.random.standard_normal((N, D_OUT, RANK)) / np.sqrt(RANK) / tn[:, None, :]),
            "W": bf(np.random.standard_normal((D_OUT, D_IN)) / np.sqrt(D_IN) / s),
            "bias": bf(np.random.standard_normal(D_OUT) * 0.3),
            "lora_weights": bf((1.0 + 0.5 * np.random.standard_normal(N)) * 2.0 / N)}


def reference(x, lora_A, lora_B, W, bias, lora_weights):
    xq = mxq(f64(x), 2, "e4m3")
    h = xq @ mxq(f64(lora_A).reshape(NR, D_IN), 1, "e4m3").T
    coef = (SCALE * f64(lora_weights))[:, None, None]
    bc = (f64(lora_B) * coef).transpose(1, 0, 2).reshape(D_OUT, NR)
    lora_out = mxq(h, 2, "e4m3") @ mxq(bc, 1, "e4m3").T
    base = (xq @ mxq(f64(W), 1, "e4m3").T) + f64(bias)
    return base + lora_out

@@ -1,0 +1,290 @@
+from contextlib import ExitStack
+
+import concourse.mybir as mybir
+from concourse.masks import make_identity
+
+F32 = mybir.dt.float32
+BF16 = mybir.dt.bfloat16
+U32 = mybir.dt.uint32
+U8 = mybir.dt.uint8
+FP8X4 = mybir.dt.float8_e4m3fn_x4
+
+P = 128
+TOKENS = 128
+D_IN = 512
+D_OUT = 1024
+ADAPTERS = 32
+RANK = 16
+LORA_SCALE = 2.0
+PACK = 4
+PAIR = 2
+HALVES = 2
+BLOCKS_PER_BANK = 2
+PSUM_BANKS = 8
+O_PER_PARTITION = D_OUT // P
+HALF_ADAPTERS = ADAPTERS // HALVES
+CHUNK_ADAPTERS = 4
+PIECES = 4
+N_TILE = D_OUT // PIECES
+ROWS_PER_PARTITION = N_TILE // P
+BIAS_ROWS = 4
+WEIGHT_ROW = BIAS_ROWS
+
+FLOPS = 2 * TOKENS * D_IN * (ADAPTERS * RANK + D_OUT) + 2 * TOKENS * ADAPTERS * RANK * D_OUT
+
+
+def banks_for(banks, blocks):
+    bank_tiles = []
+    for first in range(0, len(blocks), BLOCKS_PER_BANK):
+        bank = banks.tile([P, BLOCKS_PER_BANK, HALVES, P], F32, tag="bank")
+        bank_tiles.append(bank)
+    return bank_tiles
+
+
+def transpose_half(nc, bank_tiles, ident, blocks, u):
+    for b in range(len(blocks)):
+        bank = bank_tiles[b // BLOCKS_PER_BANK]
+        nc.tensor.transpose(bank[:, b % BLOCKS_PER_BANK, u, :], blocks[b][u], ident[:])
+
+
+def leave_banks(bank_tiles, n_blocks, places, copies):
+    for i, bank in enumerate(bank_tiles):
+        first = i * BLOCKS_PER_BANK
+        count = min(BLOCKS_PER_BANK, n_blocks - first)
+        copies[i * len(copies) // len(bank_tiles)](
+            out=places[:, :, first : first + count, :],
+            in_=bank[:, 0:count].rearrange("w b u c -> w c b u"),
+        )
+
+
+def contraction_to_partitions(nc, banks, ident, blocks, places):
+    bank_tiles = banks_for(banks, blocks)
+    for u in range(HALVES):
+        transpose_half(nc, bank_tiles, ident, blocks, u)
+    leave_banks(bank_tiles, len(blocks), places, [nc.scalar.copy])
+
+
+def row_blocks(raw):
+    words = raw[:].bitcast(F32).rearrange("p (b w u) -> p b w u", u=HALVES, w=P)
+    return [[words[:, b, :, u] for u in range(HALVES)] for b in range(words.shape[1])]
+
+
+def tile_replaced_compose_lora_pa_s_kernel(
+    tc, x, lora_A, lora_B, W, bias, lora_weights, out
+):
+    nc = tc.nc
+    with ExitStack() as stack:
+        keep = stack.enter_context(tc.tile_pool(name="keep", bufs=1))
+        banks = stack.enter_context(tc.psum_pool(name="banks", bufs=PSUM_BANKS))
+        stack.enter_context(tc.manual_schedule())
+
+        x_raw = keep.tile([TOKENS, D_IN], BF16)
+        nc.sync.dma_start(out=x_raw[:], in_=x.flatten_outer_dims())
+        small_rows = keep.tile([P, PAIR * P], BF16)
+        nc.vector.memset(small_rows[:].bitcast(F32), 0.0)
+        nc.sync.dma_start(
+            out=small_rows[WEIGHT_ROW : WEIGHT_ROW + 1, 0:ADAPTERS],
+            in_=lora_weights.rearrange("(o n) -> o n", o=1),
+        )
+        nc.sync.dma_start(
+            out=small_rows[0:BIAS_ROWS, :], in_=bias.rearrange("(i c) -> i c", i=BIAS_ROWS)
+        )
+        a_raw = keep.tile([P, PACK * D_IN], BF16)
+        nc.sync.dma_start(
+            out=a_raw[:],
+            in_=lora_A.flatten_outer_dims().rearrange("(w t) d -> w (t d)", t=PACK),
+        )
+        b_raw = []
+        for first in range(0, ADAPTERS, CHUNK_ADAPTERS):
+            chunk = keep.tile(
+                [P, CHUNK_ADAPTERS, O_PER_PARTITION * RANK], BF16, name="b_raw%d" % first
+            )
+            nc.sync.dma_start(
+                out=chunk[:],
+                in_=lora_B[first : first + CHUNK_ADAPTERS].rearrange(
+                    "n (p l) r -> p n (l r)", l=O_PER_PARTITION
+                ),
+            )
+            b_raw.append(chunk)
+        w_raw = []
+        for g in range(PIECES):
+            piece = keep.tile([P, ROWS_PER_PARTITION * D_IN], BF16, name="w_raw%d" % g)
+            nc.sync.dma_start(
+                out=piece[:],
+                in_=W[g * N_TILE : (g + 1) * N_TILE, :].rearrange(
+                    "(q j) d -> q (j d)", j=ROWS_PER_PARTITION
+                ),
+            )
+            w_raw.append(piece)
+
+        ident = keep.tile([P, P], F32)
+        make_identity(nc, ident[:])
+
+        x_grouped = keep.tile([P, TOKENS * PACK], BF16, align_bytes=64)
+        contraction_to_partitions(
+            nc,
+            banks,
+            ident,
+            row_blocks(x_raw),
+            x_grouped[:].bitcast(F32).rearrange("w (b c u) -> w c b u", b=1, u=HALVES),
+        )
+
+        small_bank = banks.tile([P, P], F32, tag="bank")
+        nc.tensor.transpose(small_bank[:], small_rows[:].bitcast(F32), ident[:])
+        small_columns = keep.tile([P, WEIGHT_ROW + 1], F32)
+        nc.vector.tensor_copy(out=small_columns[:], in_=small_bank[:, 0 : WEIGHT_ROW + 1])
+        weight_bank = banks.tile([P, P], F32, tag="bank")
+        nc.tensor.transpose(
+            weight_bank[:],
+            small_columns[:, WEIGHT_ROW : WEIGHT_ROW + 1].to_broadcast([P, P]),
+            ident[:],
+        )
+        coef = keep.tile([P, ADAPTERS, RANK], BF16)
+        nc.vector.tensor_scalar_mul(
+            out=coef[:],
+            in0=weight_bank[:, 0 : ADAPTERS // PAIR]
+            .bitcast(BF16)
+            .unsqueeze(2)
+            .to_broadcast([P, ADAPTERS, RANK]),
+            scalar1=LORA_SCALE,
+        )
+        x_codes = keep.tile([P, TOKENS], U32, align_bytes=64)
+        x_scales = keep.tile([P, TOKENS], U8, align_bytes=64)
+        nc.vector.quantize_mx(out=x_codes[:].bitcast(FP8X4), scales=x_scales[:], in_=x_grouped[:])
+
+        a_grouped = keep.tile([P, PACK * P * PACK], BF16, align_bytes=64)
+        contraction_to_partitions(
+            nc,
+            banks,
+            ident,
+            row_blocks(a_raw),
+            a_grouped[:].bitcast(F32).rearrange("w (b c u) -> w c b u", b=PACK, u=HALVES),
+        )
+
+        bias_bank = banks.tile([P, BIAS_ROWS, P], F32, tag="bank")
+        for i in range(BIAS_ROWS):
+            nc.tensor.transpose(
+                bias_bank[:, i, :], small_columns[:, i : i + 1].to_broadcast([P, P]), ident[:]
+            )
+        bias_all = keep.tile([P, D_OUT], BF16)
+        nc.scalar.copy(
+            out=bias_all[:].bitcast(F32), in_=bias_bank[:].rearrange("p i w -> p (i w)")
+        )
+
+        bc = keep.tile([P, O_PER_PARTITION * ADAPTERS * RANK], BF16)
+        bc_blocks = row_blocks(bc)
+        bc_banks = banks_for(banks, bc_blocks)
+
+        def scale_half(u):
+            for in_half in range(0, HALF_ADAPTERS, CHUNK_ADAPTERS):
+                first = u * HALF_ADAPTERS + in_half
+                nc.vector.tensor_tensor(
+                    out=bc[:].rearrange("p (l n r) -> p l n r", l=O_PER_PARTITION, r=RANK)[
+                        :, :, first : first + CHUNK_ADAPTERS, :
+                    ],
+                    in0=b_raw[first // CHUNK_ADAPTERS][:].rearrange("p n (l r) -> p l n r", r=RANK),
+                    in1=coef[:, first : first + CHUNK_ADAPTERS, :]
+                    .unsqueeze(1)
+                    .to_broadcast([P, O_PER_PARTITION, CHUNK_ADAPTERS, RANK]),
+                    op=mybir.AluOpType.mult,
+                )
+
+        scale_half(0)
+
+        a_codes = keep.tile([P, PACK * P], U32, align_bytes=64)
+        a_scales = keep.tile([P, PACK * P], U8, align_bytes=64)
+        nc.vector.quantize_mx(out=a_codes[:].bitcast(FP8X4), scales=a_scales[:], in_=a_grouped[:])
+        h_bank = banks.tile([P, PACK, TOKENS], F32, tag="bank")
+        for t in range(PACK):
+            nc.tensor.matmul_mx(
+                out=h_bank[:, t, :],
+                lhsT=a_codes[:, t * P : (t + 1) * P].bitcast(FP8X4),
+                lhsT_scale=a_scales[:, t * P : (t + 1) * P],
+                rhs=x_codes[:].bitcast(FP8X4),
+                rhs_scale=x_scales[:],
+                start=True,
+                stop=True,
+            )
+        h_grouped = keep.tile([P, TOKENS * PACK], BF16, align_bytes=64)
+        nc.scalar.copy(
+            out=h_grouped[:].rearrange("w (s t) -> w s t", t=PACK),
+            in_=h_bank[:].rearrange("w t s -> w s t"),
+        )
+
+        scale_half(1)
+        for u in range(HALVES):
+            transpose_half(nc, bc_banks, ident, bc_blocks, u)
+
+        h_codes = keep.tile([P, TOKENS], U32, align_bytes=64)
+        h_scales = keep.tile([P, TOKENS], U8, align_bytes=64)
+        nc.vector.quantize_mx(out=h_codes[:].bitcast(FP8X4), scales=h_scales[:], in_=h_grouped[:])
+
+        b_grouped = keep.tile([P, D_OUT * PACK], BF16, align_bytes=64)
+        leave_banks(
+            bc_banks,
+            len(bc_blocks),
+            b_grouped[:].bitcast(F32).rearrange("w (c b u) -> w c b u", b=O_PER_PARTITION, u=HALVES),
+            [nc.scalar.copy, nc.vector.tensor_copy],
+        )
+
+        w_grouped = keep.tile([P, D_OUT * PACK], BF16, align_bytes=64)
+        for g in range(PIECES):
+            contraction_to_partitions(
+                nc,
+                banks,
+                ident,
+                row_blocks(w_raw[g]),
+                w_grouped[:, g * N_TILE * PACK : (g + 1) * N_TILE * PACK]
+                .bitcast(F32)
+                .rearrange("w (c b u) -> w c b u", b=ROWS_PER_PARTITION, u=HALVES),
+            )
+
+        b_codes = keep.tile([P, D_OUT], U32, align_bytes=64)
+        b_scales = keep.tile([P, D_OUT], U8, align_bytes=64)
+        acc = []
+        for g in range(PIECES):
+            cols = slice(g * N_TILE, (g + 1) * N_TILE)
+            nc.vector.quantize_mx(
+                out=b_codes[:, cols].bitcast(FP8X4),
+                scales=b_scales[:, cols],
+                in_=b_grouped[:, g * N_TILE * PACK : (g + 1) * N_TILE * PACK],
+            )
+            sums = banks.tile([TOKENS, N_TILE], F32, tag="bank", name="acc%d" % g)
+            nc.tensor.matmul_mx(
+                out=sums[:],
+                lhsT=h_codes[:].bitcast(FP8X4),
+                lhsT_scale=h_scales[:],
+                rhs=b_codes[:, cols].bitcast(FP8X4),
+                rhs_scale=b_scales[:, cols],
+                start=True,
+                stop=False,
+            )
+            acc.append(sums)
+
+        w_codes = keep.tile([P, D_OUT], U32, align_bytes=64)
+        w_scales = keep.tile([P, D_OUT], U8, align_bytes=64)
+        for g in range(PIECES):
+            cols = slice(g * N_TILE, (g + 1) * N_TILE)
+            nc.vector.quantize_mx(
+                out=w_codes[:, cols].bitcast(FP8X4),
+                scales=w_scales[:, cols],
+                in_=w_grouped[:, g * N_TILE * PACK : (g + 1) * N_TILE * PACK],
+            )
+
+        out_sb = keep.tile([TOKENS, D_OUT], F32)
+        out_rows = out.flatten_outer_dims()
+        for g in range(PIECES):
+            cols = slice(g * N_TILE, (g + 1) * N_TILE)
+            nc.tensor.matmul_mx(
+                out=acc[g][:],
+                lhsT=x_codes[:].bitcast(FP8X4),
+                lhsT_scale=x_scales[:],
+                rhs=w_codes[:, cols].bitcast(FP8X4),
+                rhs_scale=w_scales[:, cols],
+                start=False,
+                stop=True,
+            )
+            nc.vector.tensor_tensor(
+                out=out_sb[:, cols], in0=acc[g][:], in1=bias_all[:, cols], op=mybir.AluOpType.add
+            )
+            nc.sync.dma_start(out=out_rows[:, cols], in_=out_sb[:, cols])

@@ -18,55 +18,18 @@ RANK = 16
 LORA_SCALE = 2.0
 PACK = 4
 PAIR = 2
-HALVES = 2
-BLOCKS_PER_BANK = 2
 PSUM_BANKS = 8
-O_PER_PARTITION = D_OUT // P
-HALF_ADAPTERS = ADAPTERS // HALVES
-CHUNK_ADAPTERS = 4
+HALF = P // 2
+L = D_OUT // HALF
+N_PAIRS = ADAPTERS // PAIR
+CHUNK = 4
+L_BANK = 4
 PIECES = 4
 N_TILE = D_OUT // PIECES
 ROWS_PER_PARTITION = N_TILE // P
 BIAS_ROWS = 4
-WEIGHT_ROW = BIAS_ROWS
 
 FLOPS = 2 * TOKENS * D_IN * (ADAPTERS * RANK + D_OUT) + 2 * TOKENS * ADAPTERS * RANK * D_OUT
-
-
-def banks_for(banks, blocks):
-    bank_tiles = []
-    for first in range(0, len(blocks), BLOCKS_PER_BANK):
-        bank = banks.tile([P, BLOCKS_PER_BANK, HALVES, P], F32, tag="bank")
-        bank_tiles.append(bank)
-    return bank_tiles
-
-
-def transpose_half(nc, bank_tiles, ident, blocks, u):
-    for b in range(len(blocks)):
-        bank = bank_tiles[b // BLOCKS_PER_BANK]
-        nc.tensor.transpose(bank[:, b % BLOCKS_PER_BANK, u, :], blocks[b][u], ident[:])
-
-
-def leave_banks(bank_tiles, n_blocks, places, copies):
-    for i, bank in enumerate(bank_tiles):
-        first = i * BLOCKS_PER_BANK
-        count = min(BLOCKS_PER_BANK, n_blocks - first)
-        copies[i * len(copies) // len(bank_tiles)](
-            out=places[:, :, first : first + count, :],
-            in_=bank[:, 0:count].rearrange("w b u c -> w c b u"),
-        )
-
-
-def contraction_to_partitions(nc, banks, ident, blocks, places):
-    bank_tiles = banks_for(banks, blocks)
-    for u in range(HALVES):
-        transpose_half(nc, bank_tiles, ident, blocks, u)
-    leave_banks(bank_tiles, len(blocks), places, [nc.scalar.copy])
-
-
-def row_blocks(raw):
-    words = raw[:].bitcast(F32).rearrange("p (b w u) -> p b w u", u=HALVES, w=P)
-    return [[words[:, b, :, u] for u in range(HALVES)] for b in range(words.shape[1])]
 
 
 def tile_replaced_compose_lora_pa_s_kernel(
@@ -80,31 +43,25 @@ def tile_replaced_compose_lora_pa_s_kernel(
 
         x_raw = keep.tile([TOKENS, D_IN], BF16)
         nc.sync.dma_start(out=x_raw[:], in_=x.flatten_outer_dims())
+        weight_rows = keep.tile([P, ADAPTERS], BF16)
+        nc.vector.memset(weight_rows[:].bitcast(F32), 0.0)
+        nc.sync.dma_start(
+            out=weight_rows[0:1, :], in_=lora_weights.rearrange("(o n) -> o n", o=1)
+        )
         small_rows = keep.tile([P, PAIR * P], BF16)
         nc.vector.memset(small_rows[:].bitcast(F32), 0.0)
-        nc.sync.dma_start(
-            out=small_rows[WEIGHT_ROW : WEIGHT_ROW + 1, 0:ADAPTERS],
-            in_=lora_weights.rearrange("(o n) -> o n", o=1),
-        )
         nc.sync.dma_start(
             out=small_rows[0:BIAS_ROWS, :], in_=bias.rearrange("(i c) -> i c", i=BIAS_ROWS)
         )
         a_raw = keep.tile([P, PACK * D_IN], BF16)
         nc.sync.dma_start(
-            out=a_raw[:],
-            in_=lora_A.flatten_outer_dims().rearrange("(w t) d -> w (t d)", t=PACK),
+            out=a_raw[:], in_=lora_A.flatten_outer_dims().rearrange("(m s) d -> m (s d)", s=PACK)
         )
         b_raw = []
-        for first in range(0, ADAPTERS, CHUNK_ADAPTERS):
-            chunk = keep.tile(
-                [P, CHUNK_ADAPTERS, O_PER_PARTITION * RANK], BF16, name="b_raw%d" % first
-            )
-            nc.sync.dma_start(
-                out=chunk[:],
-                in_=lora_B[first : first + CHUNK_ADAPTERS].rearrange(
-                    "n (p l) r -> p n (l r)", l=O_PER_PARTITION
-                ),
-            )
+        b_view = lora_B.rearrange("(q z) (p l) r -> (z p) q (l r)", z=PAIR, l=L)
+        for first in range(0, N_PAIRS, CHUNK):
+            chunk = keep.tile([P, CHUNK, L * RANK], BF16, name="b_raw%d" % first)
+            nc.sync.dma_start(out=chunk[:], in_=b_view[:, first : first + CHUNK, :])
             b_raw.append(chunk)
         w_raw = []
         for g in range(PIECES):
@@ -112,54 +69,87 @@ def tile_replaced_compose_lora_pa_s_kernel(
             nc.sync.dma_start(
                 out=piece[:],
                 in_=W[g * N_TILE : (g + 1) * N_TILE, :].rearrange(
-                    "(q j) d -> q (j d)", j=ROWS_PER_PARTITION
+                    "(c j) d -> c (j d)", j=ROWS_PER_PARTITION
                 ),
             )
             w_raw.append(piece)
 
         ident = keep.tile([P, P], F32)
         make_identity(nc, ident[:])
+        select = keep.tile([P, 3 * HALF], BF16)
+        nc.vector.memset(select[:, 0:HALF], 0.0)
+        nc.vector.memset(select[:, HALF : 2 * HALF], LORA_SCALE)
+        nc.vector.memset(select[:, 2 * HALF : 3 * HALF], 0.0)
+        perm = keep.tile([P, P], F32)
+        nc.vector.tensor_copy(
+            out=perm[:].rearrange("p (z q v) -> p z q v", z=PAIR, q=N_PAIRS),
+            in_=ident[:].rearrange("p (q z v) -> p z q v", z=PAIR, q=N_PAIRS),
+        )
+
+        def d_words(raw, rows):
+            return raw[:].bitcast(F32).rearrange("p (b w u) -> p b u w", b=rows, u=PAIR)
 
         x_grouped = keep.tile([P, TOKENS * PACK], BF16, align_bytes=64)
-        contraction_to_partitions(
-            nc,
-            banks,
-            ident,
-            row_blocks(x_raw),
-            x_grouped[:].bitcast(F32).rearrange("w (b c u) -> w c b u", b=1, u=HALVES),
+        x_bank = banks.tile([P, PAIR, P], F32, tag="bank")
+        for u in range(PAIR):
+            nc.tensor.transpose(x_bank[:, u, :], d_words(x_raw, 1)[:, 0, u, :], ident[:])
+        nc.scalar.copy(
+            out=x_grouped[:].bitcast(F32).rearrange("w (c u) -> w c u", u=PAIR),
+            in_=x_bank[:].rearrange("w u c -> w c u"),
         )
 
-        small_bank = banks.tile([P, P], F32, tag="bank")
-        nc.tensor.transpose(small_bank[:], small_rows[:].bitcast(F32), ident[:])
-        small_columns = keep.tile([P, WEIGHT_ROW + 1], F32)
-        nc.vector.tensor_copy(out=small_columns[:], in_=small_bank[:, 0 : WEIGHT_ROW + 1])
-        weight_bank = banks.tile([P, P], F32, tag="bank")
-        nc.tensor.transpose(
-            weight_bank[:],
-            small_columns[:, WEIGHT_ROW : WEIGHT_ROW + 1].to_broadcast([P, P]),
-            ident[:],
-        )
-        coef = keep.tile([P, ADAPTERS, RANK], BF16)
-        nc.vector.tensor_scalar_mul(
-            out=coef[:],
-            in0=weight_bank[:, 0 : ADAPTERS // PAIR]
-            .bitcast(BF16)
-            .unsqueeze(2)
-            .to_broadcast([P, ADAPTERS, RANK]),
-            scalar1=LORA_SCALE,
-        )
+        coef_bank = banks.tile([P, N_PAIRS], F32, tag="bank")
+        for z in range(PAIR):
+            nc.tensor.matmul(
+                coef_bank[:],
+                lhsT=select[:, HALF * (1 - z) : HALF * (1 - z) + P],
+                rhs=weight_rows[:].rearrange("p (q z) -> p z q", z=PAIR)[:, z, :],
+                start=(z == 0),
+                stop=(z == 1),
+            )
+        coef = keep.tile([P, N_PAIRS], F32)
+        nc.scalar.copy(out=coef[:], in_=coef_bank[:])
+
         x_codes = keep.tile([P, TOKENS], U32, align_bytes=64)
         x_scales = keep.tile([P, TOKENS], U8, align_bytes=64)
         nc.vector.quantize_mx(out=x_codes[:].bitcast(FP8X4), scales=x_scales[:], in_=x_grouped[:])
 
+        bc = keep.tile([P, L, N_PAIRS * RANK], BF16)
+
+        def scale_chunk(i):
+            first = i * CHUNK
+            for q in range(first, first + CHUNK):
+                nc.vector.tensor_scalar_mul(
+                    out=bc[:, :, q * RANK : (q + 1) * RANK],
+                    in0=b_raw[i][:, q - first, :].rearrange("p (l r) -> p l r", r=RANK),
+                    scalar1=coef[:, q : q + 1],
+                )
+
+        scale_chunk(0)
+        small_bank = banks.tile([P, P], F32, tag="bank")
+        nc.tensor.transpose(small_bank[:], small_rows[:].bitcast(F32), ident[:])
+        small_columns = keep.tile([P, BIAS_ROWS], F32)
+        nc.vector.tensor_copy(out=small_columns[:], in_=small_bank[:, 0:BIAS_ROWS])
+
+        scale_chunk(1)
+        scale_chunk(2)
+        scale_chunk(3)
+
         a_grouped = keep.tile([P, PACK * P * PACK], BF16, align_bytes=64)
-        contraction_to_partitions(
-            nc,
-            banks,
-            ident,
-            row_blocks(a_raw),
-            a_grouped[:].bitcast(F32).rearrange("w (b c u) -> w c b u", b=PACK, u=HALVES),
-        )
+        a_words = d_words(a_raw, PACK)
+        for e in range(PAIR):
+            bank = banks.tile([P, PAIR, PAIR, P], F32, tag="bank")
+            for vl in range(PAIR):
+                for u in range(PAIR):
+                    nc.tensor.transpose(
+                        bank[:, vl, u, :], a_words[:, PAIR * vl + e, u, :], perm[:]
+                    )
+            nc.scalar.copy(
+                out=a_grouped[:, e * PAIR * P * PACK : (e + 1) * PAIR * P * PACK]
+                .bitcast(F32)
+                .rearrange("w (c v u) -> w c v u", v=PAIR, u=PAIR),
+                in_=bank[:].rearrange("w v u c -> w c v u"),
+            )
 
         bias_bank = banks.tile([P, BIAS_ROWS, P], F32, tag="bank")
         for i in range(BIAS_ROWS):
@@ -171,72 +161,72 @@ def tile_replaced_compose_lora_pa_s_kernel(
             out=bias_all[:].bitcast(F32), in_=bias_bank[:].rearrange("p i w -> p (i w)")
         )
 
-        bc = keep.tile([P, O_PER_PARTITION * ADAPTERS * RANK], BF16)
-        bc_blocks = row_blocks(bc)
-        bc_banks = banks_for(banks, bc_blocks)
-
-        def scale_half(u):
-            for in_half in range(0, HALF_ADAPTERS, CHUNK_ADAPTERS):
-                first = u * HALF_ADAPTERS + in_half
-                nc.vector.tensor_tensor(
-                    out=bc[:].rearrange("p (l n r) -> p l n r", l=O_PER_PARTITION, r=RANK)[
-                        :, :, first : first + CHUNK_ADAPTERS, :
-                    ],
-                    in0=b_raw[first // CHUNK_ADAPTERS][:].rearrange("p n (l r) -> p l n r", r=RANK),
-                    in1=coef[:, first : first + CHUNK_ADAPTERS, :]
-                    .unsqueeze(1)
-                    .to_broadcast([P, O_PER_PARTITION, CHUNK_ADAPTERS, RANK]),
-                    op=mybir.AluOpType.mult,
-                )
-
-        scale_half(0)
-
         a_codes = keep.tile([P, PACK * P], U32, align_bytes=64)
         a_scales = keep.tile([P, PACK * P], U8, align_bytes=64)
         nc.vector.quantize_mx(out=a_codes[:].bitcast(FP8X4), scales=a_scales[:], in_=a_grouped[:])
-        h_bank = banks.tile([P, PACK, TOKENS], F32, tag="bank")
-        for t in range(PACK):
-            nc.tensor.matmul_mx(
-                out=h_bank[:, t, :],
-                lhsT=a_codes[:, t * P : (t + 1) * P].bitcast(FP8X4),
-                lhsT_scale=a_scales[:, t * P : (t + 1) * P],
-                rhs=x_codes[:].bitcast(FP8X4),
-                rhs_scale=x_scales[:],
-                start=True,
-                stop=True,
+
+        b_grouped = keep.tile([P, D_OUT * PACK], BF16, align_bytes=64)
+        b_places = b_grouped[:].bitcast(F32).rearrange("w (p l z) -> w p l z", l=L, z=PAIR)
+        bc_words = bc[:].rearrange("p l c -> p (l c)").bitcast(F32).rearrange("p (l w) -> p l w", w=P)
+        def transpose_bc(first):
+            bank = banks.tile([P, L_BANK, PAIR, HALF], F32, tag="bank", name="bc_bank%d" % first)
+            for l in range(L_BANK):
+                nc.tensor.transpose(
+                    bank[:, l].rearrange("w z p -> w (z p)"), bc_words[:, first + l, :], ident[:]
+                )
+            return bank
+
+        def leave_bc(first, bank, copy):
+            copy(
+                out=b_places[:, :, first : first + L_BANK, :],
+                in_=bank[:].rearrange("w l z p -> w p l z"),
             )
+
+        bank0 = transpose_bc(0)
+        bank1 = transpose_bc(4)
+        leave_bc(0, bank0, nc.scalar.copy)
+        leave_bc(4, bank1, nc.vector.tensor_copy)
+
+        h_bank = banks.tile([P, PAIR, PAIR, TOKENS], F32, tag="bank")
+        for e in range(PAIR):
+            for z in range(PAIR):
+                cols = slice((PAIR * e + z) * P, (PAIR * e + z + 1) * P)
+                nc.tensor.matmul_mx(
+                    out=h_bank[:, e, z, :],
+                    lhsT=a_codes[:, cols].bitcast(FP8X4),
+                    lhsT_scale=a_scales[:, cols],
+                    rhs=x_codes[:].bitcast(FP8X4),
+                    rhs_scale=x_scales[:],
+                    start=True,
+                    stop=True,
+                )
         h_grouped = keep.tile([P, TOKENS * PACK], BF16, align_bytes=64)
         nc.scalar.copy(
-            out=h_grouped[:].rearrange("w (s t) -> w s t", t=PACK),
-            in_=h_bank[:].rearrange("w t s -> w s t"),
+            out=h_grouped[:].rearrange("w (s z e) -> w s z e", z=PAIR, e=PAIR),
+            in_=h_bank[:].rearrange("w e z s -> w s z e"),
         )
-
-        scale_half(1)
-        for u in range(HALVES):
-            transpose_half(nc, bc_banks, ident, bc_blocks, u)
 
         h_codes = keep.tile([P, TOKENS], U32, align_bytes=64)
         h_scales = keep.tile([P, TOKENS], U8, align_bytes=64)
         nc.vector.quantize_mx(out=h_codes[:].bitcast(FP8X4), scales=h_scales[:], in_=h_grouped[:])
 
-        b_grouped = keep.tile([P, D_OUT * PACK], BF16, align_bytes=64)
-        leave_banks(
-            bc_banks,
-            len(bc_blocks),
-            b_grouped[:].bitcast(F32).rearrange("w (c b u) -> w c b u", b=O_PER_PARTITION, u=HALVES),
-            [nc.scalar.copy, nc.vector.tensor_copy],
-        )
+        bank2 = transpose_bc(8)
+        bank3 = transpose_bc(12)
+        leave_bc(8, bank2, nc.scalar.copy)
+        leave_bc(12, bank3, nc.vector.tensor_copy)
 
         w_grouped = keep.tile([P, D_OUT * PACK], BF16, align_bytes=64)
         for g in range(PIECES):
-            contraction_to_partitions(
-                nc,
-                banks,
-                ident,
-                row_blocks(w_raw[g]),
-                w_grouped[:, g * N_TILE * PACK : (g + 1) * N_TILE * PACK]
+            words = d_words(w_raw[g], ROWS_PER_PARTITION)
+            bank = banks.tile([P, ROWS_PER_PARTITION, PAIR, P], F32, tag="bank")
+            for j in range(ROWS_PER_PARTITION):
+                for u in range(PAIR):
+                    nc.tensor.transpose(bank[:, j, u, :], words[:, j, u, :], ident[:])
+            nc.scalar.copy(
+                out=w_grouped[:, g * N_TILE * PACK : (g + 1) * N_TILE * PACK]
                 .bitcast(F32)
-                .rearrange("w (c b u) -> w c b u", b=ROWS_PER_PARTITION, u=HALVES),
+                .rearrange("w (c j u) -> w c j u", j=ROWS_PER_PARTITION, u=PAIR),
+                in_=bank[:].rearrange("w j u c -> w c j u"),
             )
 
         b_codes = keep.tile([P, D_OUT], U32, align_bytes=64)
@@ -263,18 +253,16 @@ def tile_replaced_compose_lora_pa_s_kernel(
 
         w_codes = keep.tile([P, D_OUT], U32, align_bytes=64)
         w_scales = keep.tile([P, D_OUT], U8, align_bytes=64)
-        for g in range(PIECES):
+        out_sb = keep.tile([TOKENS, D_OUT], F32)
+        out_rows = out.flatten_outer_dims()
+
+        def quantise_w(g):
             cols = slice(g * N_TILE, (g + 1) * N_TILE)
             nc.vector.quantize_mx(
                 out=w_codes[:, cols].bitcast(FP8X4),
                 scales=w_scales[:, cols],
                 in_=w_grouped[:, g * N_TILE * PACK : (g + 1) * N_TILE * PACK],
             )
-
-        out_sb = keep.tile([TOKENS, D_OUT], F32)
-        out_rows = out.flatten_outer_dims()
-        for g in range(PIECES):
-            cols = slice(g * N_TILE, (g + 1) * N_TILE)
             nc.tensor.matmul_mx(
                 out=acc[g][:],
                 lhsT=x_codes[:].bitcast(FP8X4),
@@ -284,7 +272,16 @@ def tile_replaced_compose_lora_pa_s_kernel(
                 start=False,
                 stop=True,
             )
+
+        def finish(g):
+            cols = slice(g * N_TILE, (g + 1) * N_TILE)
             nc.vector.tensor_tensor(
                 out=out_sb[:, cols], in0=acc[g][:], in1=bias_all[:, cols], op=mybir.AluOpType.add
             )
             nc.sync.dma_start(out=out_rows[:, cols], in_=out_sb[:, cols])
+
+        for g in range(PIECES):
+            quantise_w(g)
+            if g > 0:
+                finish(g - 1)
+        finish(PIECES - 1)

@@ -263,6 +263,9 @@ def tile_replaced_compose_lora_pa_s_kernel(
                 scales=w_scales[:, cols],
                 in_=w_grouped[:, g * N_TILE * PACK : (g + 1) * N_TILE * PACK],
             )
+
+        def finish(g):
+            cols = slice(g * N_TILE, (g + 1) * N_TILE)
             nc.tensor.matmul_mx(
                 out=acc[g][:],
                 lhsT=x_codes[:].bitcast(FP8X4),
@@ -272,9 +275,6 @@ def tile_replaced_compose_lora_pa_s_kernel(
                 start=False,
                 stop=True,
             )
-
-        def finish(g):
-            cols = slice(g * N_TILE, (g + 1) * N_TILE)
             nc.vector.tensor_tensor(
                 out=out_sb[:, cols], in0=acc[g][:], in1=bias_all[:, cols], op=mybir.AluOpType.add
             )
@@ -282,6 +282,5 @@ def tile_replaced_compose_lora_pa_s_kernel(
 
         for g in range(PIECES):
             quantise_w(g)
-            if g > 0:
-                finish(g - 1)
-        finish(PIECES - 1)
+        for g in range(PIECES):
+            finish(g)

@@ -132,8 +132,6 @@ def tile_replaced_compose_lora_pa_s_kernel(
         nc.vector.tensor_copy(out=small_columns[:], in_=small_bank[:, 0:BIAS_ROWS])
 
         scale_chunk(1)
-        scale_chunk(2)
-        scale_chunk(3)
 
         a_grouped = keep.tile([P, PACK * P * PACK], BF16, align_bytes=64)
         a_words = d_words(a_raw, PACK)
@@ -164,6 +162,27 @@ def tile_replaced_compose_lora_pa_s_kernel(
         a_codes = keep.tile([P, PACK * P], U32, align_bytes=64)
         a_scales = keep.tile([P, PACK * P], U8, align_bytes=64)
         nc.vector.quantize_mx(out=a_codes[:].bitcast(FP8X4), scales=a_scales[:], in_=a_grouped[:])
+        h_bank = banks.tile([P, PAIR, PAIR, TOKENS], F32, tag="bank")
+        for e in range(PAIR):
+            for z in range(PAIR):
+                cols = slice((PAIR * e + z) * P, (PAIR * e + z + 1) * P)
+                nc.tensor.matmul_mx(
+                    out=h_bank[:, e, z, :],
+                    lhsT=a_codes[:, cols].bitcast(FP8X4),
+                    lhsT_scale=a_scales[:, cols],
+                    rhs=x_codes[:].bitcast(FP8X4),
+                    rhs_scale=x_scales[:],
+                    start=True,
+                    stop=True,
+                )
+        h_grouped = keep.tile([P, TOKENS * PACK], BF16, align_bytes=64)
+        nc.scalar.copy(
+            out=h_grouped[:].rearrange("w (s z e) -> w s z e", z=PAIR, e=PAIR),
+            in_=h_bank[:].rearrange("w e z s -> w s z e"),
+        )
+
+        scale_chunk(2)
+        scale_chunk(3)
 
         b_grouped = keep.tile([P, D_OUT * PACK], BF16, align_bytes=64)
         b_places = b_grouped[:].bitcast(F32).rearrange("w (p l z) -> w p l z", l=L, z=PAIR)
@@ -186,26 +205,6 @@ def tile_replaced_compose_lora_pa_s_kernel(
         bank1 = transpose_bc(4)
         leave_bc(0, bank0, nc.scalar.copy)
         leave_bc(4, bank1, nc.vector.tensor_copy)
-
-        h_bank = banks.tile([P, PAIR, PAIR, TOKENS], F32, tag="bank")
-        for e in range(PAIR):
-            for z in range(PAIR):
-                cols = slice((PAIR * e + z) * P, (PAIR * e + z + 1) * P)
-                nc.tensor.matmul_mx(
-                    out=h_bank[:, e, z, :],
-                    lhsT=a_codes[:, cols].bitcast(FP8X4),
-                    lhsT_scale=a_scales[:, cols],
-                    rhs=x_codes[:].bitcast(FP8X4),
-                    rhs_scale=x_scales[:],
-                    start=True,
-                    stop=True,
-                )
-        h_grouped = keep.tile([P, TOKENS * PACK], BF16, align_bytes=64)
-        nc.scalar.copy(
-            out=h_grouped[:].rearrange("w (s z e) -> w s z e", z=PAIR, e=PAIR),
-            in_=h_bank[:].rearrange("w e z s -> w s z e"),
-        )
-
         h_codes = keep.tile([P, TOKENS], U32, align_bytes=64)
         h_scales = keep.tile([P, TOKENS], U8, align_bytes=64)
         nc.vector.quantize_mx(out=h_codes[:].bitcast(FP8X4), scales=h_scales[:], in_=h_grouped[:])

@@ -38,7 +38,8 @@ def tile_replaced_compose_lora_pa_s_kernel(
     nc = tc.nc
     with ExitStack() as stack:
         keep = stack.enter_context(tc.tile_pool(name="keep", bufs=1))
-        banks = stack.enter_context(tc.psum_pool(name="banks", bufs=PSUM_BANKS))
+        banks = stack.enter_context(tc.psum_pool(name="banks", bufs=PSUM_BANKS - 1))
+        spare = stack.enter_context(tc.psum_pool(name="spare", bufs=1))
         stack.enter_context(tc.manual_schedule())
 
         x_raw = keep.tile([TOKENS, D_IN], BF16)
@@ -86,6 +87,26 @@ def tile_replaced_compose_lora_pa_s_kernel(
             in_=ident[:].rearrange("p (q z v) -> p z q v", z=PAIR, q=N_PAIRS),
         )
 
+        warm = spare.tile([P, 4 * P], F32)
+
+        def busy_plain(n):
+            for i in range(n):
+                nc.tensor.matmul(warm[:, 0:P], lhsT=ident[:], rhs=ident[:], start=True, stop=True)
+
+        def busy_mx(n, codes, scales):
+            for i in range(n):
+                nc.tensor.matmul_mx(
+                    out=warm[:, 0 : codes.shape[1]],
+                    lhsT=x_codes[:].bitcast(FP8X4),
+                    lhsT_scale=x_scales[:],
+                    rhs=codes[:].bitcast(FP8X4),
+                    rhs_scale=scales[:],
+                    start=True,
+                    stop=True,
+                )
+
+        busy_plain(3)
+
         def d_words(raw, rows):
             return raw[:].bitcast(F32).rearrange("p (b w u) -> p b u w", b=rows, u=PAIR)
 
@@ -128,6 +149,7 @@ def tile_replaced_compose_lora_pa_s_kernel(
         scale_chunk(0)
         small_bank = banks.tile([P, P], F32, tag="bank")
         nc.tensor.transpose(small_bank[:], small_rows[:].bitcast(F32), ident[:])
+        busy_plain(2)
         small_columns = keep.tile([P, BIAS_ROWS], F32)
         nc.vector.tensor_copy(out=small_columns[:], in_=small_bank[:, 0:BIAS_ROWS])
 
@@ -149,6 +171,8 @@ def tile_replaced_compose_lora_pa_s_kernel(
                 in_=bank[:].rearrange("w v u c -> w c v u"),
             )
 
+        busy_mx(8, x_codes, x_scales)
+
         bias_bank = banks.tile([P, BIAS_ROWS, P], F32, tag="bank")
         for i in range(BIAS_ROWS):
             nc.tensor.transpose(
@@ -162,6 +186,7 @@ def tile_replaced_compose_lora_pa_s_kernel(
         a_codes = keep.tile([P, PACK * P], U32, align_bytes=64)
         a_scales = keep.tile([P, PACK * P], U8, align_bytes=64)
         nc.vector.quantize_mx(out=a_codes[:].bitcast(FP8X4), scales=a_scales[:], in_=a_grouped[:])
+        busy_mx(4, x_codes, x_scales)
         h_bank = banks.tile([P, PAIR, PAIR, TOKENS], F32, tag="bank")
         for e in range(PAIR):
             for z in range(PAIR):
@@ -175,6 +200,7 @@ def tile_replaced_compose_lora_pa_s_kernel(
                     start=True,
                     stop=True,
                 )
+        busy_mx(1, a_codes, a_scales)
         h_grouped = keep.tile([P, TOKENS * PACK], BF16, align_bytes=64)
         nc.scalar.copy(
             out=h_grouped[:].rearrange("w (s z e) -> w s z e", z=PAIR, e=PAIR),
@@ -203,6 +229,7 @@ def tile_replaced_compose_lora_pa_s_kernel(
 
         bank0 = transpose_bc(0)
         bank1 = transpose_bc(4)
+        busy_plain(1)
         leave_bc(0, bank0, nc.scalar.copy)
         leave_bc(4, bank1, nc.vector.tensor_copy)
         h_codes = keep.tile([P, TOKENS], U32, align_bytes=64)
@@ -211,6 +238,7 @@ def tile_replaced_compose_lora_pa_s_kernel(
 
         bank2 = transpose_bc(8)
         bank3 = transpose_bc(12)
+        busy_plain(1)
         leave_bc(8, bank2, nc.scalar.copy)
         leave_bc(12, bank3, nc.vector.tensor_copy)
 

from contextlib import ExitStack

import concourse.mybir as mybir
from concourse.masks import make_identity

F32 = mybir.dt.float32
BF16 = mybir.dt.bfloat16
U32 = mybir.dt.uint32
U8 = mybir.dt.uint8
FP8X4 = mybir.dt.float8_e4m3fn_x4

P = 128
TOKENS = 128
D_IN = 512
D_OUT = 1024
ADAPTERS = 32
RANK = 16
LORA_SCALE = 2.0
PACK = 4
PAIR = 2
PSUM_BANKS = 8
HALF = P // 2
L = D_OUT // HALF
N_PAIRS = ADAPTERS // PAIR
CHUNK = 4
L_BANK = 4
PIECES = 4
N_TILE = D_OUT // PIECES
ROWS_PER_PARTITION = N_TILE // P
BIAS_ROWS = 4

FLOPS = 2 * TOKENS * D_IN * (ADAPTERS * RANK + D_OUT) + 2 * TOKENS * ADAPTERS * RANK * D_OUT


def tile_replaced_compose_lora_pa_s_kernel(
    tc, x, lora_A, lora_B, W, bias, lora_weights, out
):
    nc = tc.nc
    with ExitStack() as stack:
        keep = stack.enter_context(tc.tile_pool(name="keep", bufs=1))
        banks = stack.enter_context(tc.psum_pool(name="banks", bufs=PSUM_BANKS - 1))
        spare = stack.enter_context(tc.psum_pool(name="spare", bufs=1))
        stack.enter_context(tc.manual_schedule())

        x_raw = keep.tile([TOKENS, D_IN], BF16)
        nc.sync.dma_start(out=x_raw[:], in_=x.flatten_outer_dims())
        weight_rows = keep.tile([P, ADAPTERS], BF16)
        nc.vector.memset(weight_rows[:].bitcast(F32), 0.0)
        nc.sync.dma_start(
            out=weight_rows[0:1, :], in_=lora_weights.rearrange("(o n) -> o n", o=1)
        )
        small_rows = keep.tile([P, PAIR * P], BF16)
        nc.vector.memset(small_rows[:].bitcast(F32), 0.0)
        nc.sync.dma_start(
            out=small_rows[0:BIAS_ROWS, :], in_=bias.rearrange("(i c) -> i c", i=BIAS_ROWS)
        )
        a_raw = keep.tile([P, PACK * D_IN], BF16)
        nc.sync.dma_start(
            out=a_raw[:], in_=lora_A.flatten_outer_dims().rearrange("(m s) d -> m (s d)", s=PACK)
        )
        b_raw = []
        b_view = lora_B.rearrange("(q z) (p l) r -> (z p) q (l r)", z=PAIR, l=L)
        for first in range(0, N_PAIRS, CHUNK):
            chunk = keep.tile([P, CHUNK, L * RANK], BF16, name="b_raw%d" % first)
            nc.sync.dma_start(out=chunk[:], in_=b_view[:, first : first + CHUNK, :])
            b_raw.append(chunk)
        w_raw = []
        for g in range(PIECES):
            piece = keep.tile([P, ROWS_PER_PARTITION * D_IN], BF16, name="w_raw%d" % g)
            nc.sync.dma_start(
                out=piece[:],
                in_=W[g * N_TILE : (g + 1) * N_TILE, :].rearrange(
                    "(c j) d -> c (j d)", j=ROWS_PER_PARTITION
                ),
            )
            w_raw.append(piece)

        ident = keep.tile([P, P], F32)
        make_identity(nc, ident[:])
        select = keep.tile([P, 3 * HALF], BF16)
        nc.vector.memset(select[:, 0:HALF], 0.0)
        nc.vector.memset(select[:, HALF : 2 * HALF], LORA_SCALE)
        nc.vector.memset(select[:, 2 * HALF : 3 * HALF], 0.0)
        perm = keep.tile([P, P], F32)
        nc.vector.tensor_copy(
            out=perm[:].rearrange("p (z q v) -> p z q v", z=PAIR, q=N_PAIRS),
            in_=ident[:].rearrange("p (q z v) -> p z q v", z=PAIR, q=N_PAIRS),
        )

        warm = spare.tile([P, 4 * P], F32)

        def busy_plain(n):
            for i in range(n):
                nc.tensor.matmul(warm[:, 0:P], lhsT=ident[:], rhs=ident[:], start=True, stop=True)

        def busy_mx(n, codes, scales):
            for i in range(n):
                nc.tensor.matmul_mx(
                    out=warm[:, 0 : codes.shape[1]],
                    lhsT=x_codes[:].bitcast(FP8X4),
                    lhsT_scale=x_scales[:],
                    rhs=codes[:].bitcast(FP8X4),
                    rhs_scale=scales[:],
                    start=True,
                    stop=True,
                )

        busy_plain(3)

        def d_words(raw, rows):
            return raw[:].bitcast(F32).rearrange("p (b w u) -> p b u w", b=rows, u=PAIR)

        x_grouped = keep.tile([P, TOKENS * PACK], BF16, align_bytes=64)
        x_bank = banks.tile([P, PAIR, P], F32, tag="bank")
        for u in range(PAIR):
            nc.tensor.transpose(x_bank[:, u, :], d_words(x_raw, 1)[:, 0, u, :], ident[:])
        nc.scalar.copy(
            out=x_grouped[:].bitcast(F32).rearrange("w (c u) -> w c u", u=PAIR),
            in_=x_bank[:].rearrange("w u c -> w c u"),
        )

        coef_bank = banks.tile([P, N_PAIRS], F32, tag="bank")
        for z in range(PAIR):
            nc.tensor.matmul(
                coef_bank[:],
                lhsT=select[:, HALF * (1 - z) : HALF * (1 - z) + P],
                rhs=weight_rows[:].rearrange("p (q z) -> p z q", z=PAIR)[:, z, :],
                start=(z == 0),
                stop=(z == 1),
            )
        coef = keep.tile([P, N_PAIRS], F32)
        nc.scalar.copy(out=coef[:], in_=coef_bank[:])

        x_codes = keep.tile([P, TOKENS], U32, align_bytes=64)
        x_scales = keep.tile([P, TOKENS], U8, align_bytes=64)
        nc.vector.quantize_mx(out=x_codes[:].bitcast(FP8X4), scales=x_scales[:], in_=x_grouped[:])

        bc = keep.tile([P, L, N_PAIRS * RANK], BF16)

        def scale_chunk(i):
            first = i * CHUNK
            for q in range(first, first + CHUNK):
                nc.vector.tensor_scalar_mul(
                    out=bc[:, :, q * RANK : (q + 1) * RANK],
                    in0=b_raw[i][:, q - first, :].rearrange("p (l r) -> p l r", r=RANK),
                    scalar1=coef[:, q : q + 1],
                )

        scale_chunk(0)
        small_bank = banks.tile([P, P], F32, tag="bank")
        nc.tensor.transpose(small_bank[:], small_rows[:].bitcast(F32), ident[:])
        busy_plain(2)
        small_columns = keep.tile([P, BIAS_ROWS], F32)
        nc.vector.tensor_copy(out=small_columns[:], in_=small_bank[:, 0:BIAS_ROWS])

        scale_chunk(1)

        a_grouped = keep.tile([P, PACK * P * PACK], BF16, align_bytes=64)
        a_words = d_words(a_raw, PACK)
        for e in range(PAIR):
            bank = banks.tile([P, PAIR, PAIR, P], F32, tag="bank")
            for vl in range(PAIR):
                for u in range(PAIR):
                    nc.tensor.transpose(
                        bank[:, vl, u, :], a_words[:, PAIR * vl + e, u, :], perm[:]
                    )
            nc.scalar.copy(
                out=a_grouped[:, e * PAIR * P * PACK : (e + 1) * PAIR * P * PACK]
                .bitcast(F32)
                .rearrange("w (c v u) -> w c v u", v=PAIR, u=PAIR),
                in_=bank[:].rearrange("w v u c -> w c v u"),
            )

        busy_mx(8, x_codes, x_scales)

        bias_bank = banks.tile([P, BIAS_ROWS, P], F32, tag="bank")
        for i in range(BIAS_ROWS):
            nc.tensor.transpose(
                bias_bank[:, i, :], small_columns[:, i : i + 1].to_broadcast([P, P]), ident[:]
            )
        bias_all = keep.tile([P, D_OUT], BF16)
        nc.scalar.copy(
            out=bias_all[:].bitcast(F32), in_=bias_bank[:].rearrange("p i w -> p (i w)")
        )

        a_codes = keep.tile([P, PACK * P], U32, align_bytes=64)
        a_scales = keep.tile([P, PACK * P], U8, align_bytes=64)
        nc.vector.quantize_mx(out=a_codes[:].bitcast(FP8X4), scales=a_scales[:], in_=a_grouped[:])
        busy_mx(4, x_codes, x_scales)
        h_bank = banks.tile([P, PAIR, PAIR, TOKENS], F32, tag="bank")
        for e in range(PAIR):
            for z in range(PAIR):
                cols = slice((PAIR * e + z) * P, (PAIR * e + z + 1) * P)
                nc.tensor.matmul_mx(
                    out=h_bank[:, e, z, :],
                    lhsT=a_codes[:, cols].bitcast(FP8X4),
                    lhsT_scale=a_scales[:, cols],
                    rhs=x_codes[:].bitcast(FP8X4),
                    rhs_scale=x_scales[:],
                    start=True,
                    stop=True,
                )
        busy_mx(1, a_codes, a_scales)
        h_grouped = keep.tile([P, TOKENS * PACK], BF16, align_bytes=64)
        nc.scalar.copy(
            out=h_grouped[:].rearrange("w (s z e) -> w s z e", z=PAIR, e=PAIR),
            in_=h_bank[:].rearrange("w e z s -> w s z e"),
        )

        scale_chunk(2)
        scale_chunk(3)

        b_grouped = keep.tile([P, D_OUT * PACK], BF16, align_bytes=64)
        b_places = b_grouped[:].bitcast(F32).rearrange("w (p l z) -> w p l z", l=L, z=PAIR)
        bc_words = bc[:].rearrange("p l c -> p (l c)").bitcast(F32).rearrange("p (l w) -> p l w", w=P)
        def transpose_bc(first):
            bank = banks.tile([P, L_BANK, PAIR, HALF], F32, tag="bank", name="bc_bank%d" % first)
            for l in range(L_BANK):
                nc.tensor.transpose(
                    bank[:, l].rearrange("w z p -> w (z p)"), bc_words[:, first + l, :], ident[:]
                )
            return bank

        def leave_bc(first, bank, copy):
            copy(
                out=b_places[:, :, first : first + L_BANK, :],
                in_=bank[:].rearrange("w l z p -> w p l z"),
            )

        bank0 = transpose_bc(0)
        bank1 = transpose_bc(4)
        busy_plain(1)
        leave_bc(0, bank0, nc.scalar.copy)
        leave_bc(4, bank1, nc.vector.tensor_copy)
        h_codes = keep.tile([P, TOKENS], U32, align_bytes=64)
        h_scales = keep.tile([P, TOKENS], U8, align_bytes=64)
        nc.vector.quantize_mx(out=h_codes[:].bitcast(FP8X4), scales=h_scales[:], in_=h_grouped[:])

        bank2 = transpose_bc(8)
        bank3 = transpose_bc(12)
        busy_plain(1)
        leave_bc(8, bank2, nc.scalar.copy)
        leave_bc(12, bank3, nc.vector.tensor_copy)

        w_grouped = keep.tile([P, D_OUT * PACK], BF16, align_bytes=64)
        for g in range(PIECES):
            words = d_words(w_raw[g], ROWS_PER_PARTITION)
            bank = banks.tile([P, ROWS_PER_PARTITION, PAIR, P], F32, tag="bank")
            for j in range(ROWS_PER_PARTITION):
                for u in range(PAIR):
                    nc.tensor.transpose(bank[:, j, u, :], words[:, j, u, :], ident[:])
            nc.scalar.copy(
                out=w_grouped[:, g * N_TILE * PACK : (g + 1) * N_TILE * PACK]
                .bitcast(F32)
                .rearrange("w (c j u) -> w c j u", j=ROWS_PER_PARTITION, u=PAIR),
                in_=bank[:].rearrange("w j u c -> w c j u"),
            )

        b_codes = keep.tile([P, D_OUT], U32, align_bytes=64)
        b_scales = keep.tile([P, D_OUT], U8, align_bytes=64)
        acc = []
        for g in range(PIECES):
            cols = slice(g * N_TILE, (g + 1) * N_TILE)
            nc.vector.quantize_mx(
                out=b_codes[:, cols].bitcast(FP8X4),
                scales=b_scales[:, cols],
                in_=b_grouped[:, g * N_TILE * PACK : (g + 1) * N_TILE * PACK],
            )
            sums = banks.tile([TOKENS, N_TILE], F32, tag="bank", name="acc%d" % g)
            nc.tensor.matmul_mx(
                out=sums[:],
                lhsT=h_codes[:].bitcast(FP8X4),
                lhsT_scale=h_scales[:],
                rhs=b_codes[:, cols].bitcast(FP8X4),
                rhs_scale=b_scales[:, cols],
                start=True,
                stop=False,
            )
            acc.append(sums)

        w_codes = keep.tile([P, D_OUT], U32, align_bytes=64)
        w_scales = keep.tile([P, D_OUT], U8, align_bytes=64)
        out_sb = keep.tile([TOKENS, D_OUT], F32)
        out_rows = out.flatten_outer_dims()

        def quantise_w(g):
            cols = slice(g * N_TILE, (g + 1) * N_TILE)
            nc.vector.quantize_mx(
                out=w_codes[:, cols].bitcast(FP8X4),
                scales=w_scales[:, cols],
                in_=w_grouped[:, g * N_TILE * PACK : (g + 1) * N_TILE * PACK],
            )

        def finish(g):
            cols = slice(g * N_TILE, (g + 1) * N_TILE)
            nc.tensor.matmul_mx(
                out=acc[g][:],
                lhsT=x_codes[:].bitcast(FP8X4),
                lhsT_scale=x_scales[:],
                rhs=w_codes[:, cols].bitcast(FP8X4),
                rhs_scale=w_scales[:, cols],
                start=False,
                stop=True,
            )
            nc.vector.tensor_tensor(
                out=out_sb[:, cols], in0=acc[g][:], in1=bias_all[:, cols], op=mybir.AluOpType.add
            )
            nc.sync.dma_start(out=out_rows[:, cols], in_=out_sb[:, cols])

        for g in range(PIECES):
            quantise_w(g)
        for g in range(PIECES):
            finish(g)
